import numpy as np
import ml_dtypes


def mxq(x, axis, fmt="e4m3"):
    dtype, down = {"e4m3": (ml_dtypes.float8_e4m3fn, 7), "e5m2": (ml_dtypes.float8_e5m2, 14)}[fmt]
    v = np.moveaxis(np.asarray(x, np.float32).astype(ml_dtypes.bfloat16).astype(np.float64), axis, -1)
    blocks = v.reshape(v.shape[:-1] + (-1, 32))
    amax = np.abs(blocks).max(-1, keepdims=True)
    byte = np.maximum(np.where(amax > 0, np.frexp(amax)[1] - 1 + 127, 0) - down, 1)
    scale = np.exp2(byte - 127.0)
    codes = (blocks / scale).astype(np.float32).astype(dtype).astype(np.float64)
    return np.moveaxis((codes * scale).reshape(v.shape), -1, axis)


WIDE = False


def mx_kscale(k):
    if not WIDE:
        return np.ones(k)
    levels = np.array([10, -10, 5, -5, 0])
    a = np.random.permutation(np.resize(levels, k // 512 * 4)).reshape(k // 512, 4)
    idx = np.arange(k)
    return np.exp2(a[idx // 512, idx % 128 // 32])


BF16 = ml_dtypes.bfloat16


def bf(x):
    return np.asarray(x, np.float32).astype(BF16)


def f64(x):
    return np.asarray(x).astype(np.float64)


B, H, W, C, NF, ZD = 128, 8, 8, 512, 256, 512
EPS = 1e-8
LRELU_SLOPE = 0.2


def setup_inputs():
    s = mx_kscale(C)
    return {"x": bf(np.random.standard_normal((B, H, W, C)) * s),
            "dlatents": bf(np.random.standard_normal((B, ZD))),
            "noise_map": bf(np.random.standard_normal((B, H, W, 1))),
            "conv_w": bf(np.random.standard_normal((C, NF)) / np.sqrt(C) / s[:, None]),
            "noise_weight": bf(np.random.standard_normal((1, 1, 1, NF)) * 0.5),
            "bias": bf(np.random.standard_normal((1, 1, 1, NF)) * 0.5),
            "dense_w": bf(np.random.standard_normal((ZD, 2 * NF)) / np.sqrt(ZD)),
            "dense_b": bf(np.random.standard_normal(2 * NF) * 0.3)}


def reference(x, dlatents, noise_map, conv_w, noise_weight, bias, dense_w, dense_b):
    y = mxq(f64(x), 3, "e4m3") @ mxq(f64(conv_w), 0, "e4m3")
    y = y + f64(noise_weight) * f64(noise_map) + f64(bias)
    y = np.where(y >= 0.0, y, LRELU_SLOPE * y)
    mu = np.mean(y, axis=(1, 2), keepdims=True)
    var = np.mean(np.square(y - mu), axis=(1, 2), keepdims=True)
    yn = (y - mu) / np.sqrt(var + EPS)
    gb = f64(dlatents) @ f64(dense_w) + f64(dense_b)
    nf = y.shape[-1]
    gb = gb.reshape(-1, 2, 1, 1, nf)
    gamma, beta = gb[:, 0], gb[:, 1]
    return yn * (1.0 + gamma) + beta

@@ -1,0 +1,372 @@
+from contextlib import ExitStack
+
+import concourse.mybir as mybir
+from concourse.masks import make_identity
+
+F32 = mybir.dt.float32
+BF16 = mybir.dt.bfloat16
+U32 = mybir.dt.uint32
+U8 = mybir.dt.uint8
+FP8X4 = mybir.dt.float8_e4m3fn_x4
+ALU = mybir.AluOpType
+ACT = mybir.ActivationFunctionType
+
+P = 128
+PIX = 8192
+CIN = 512
+NF = 256
+GP = 512
+NG = PIX // GP
+EPS = 1e-8
+SLOPE = 0.2
+FLOPS = 2 * PIX * CIN * NF + 2 * 128 * 512 * 512
+
+
+def tile_styleganlayerepilogue_t_kernel(
+    tc, x, dlatents, noise_map, conv_w, noise_weight, bias, dense_w, dense_b, out
+):
+    nc = tc.nc
+    x_rows = x.rearrange("b h w k -> (b h w) k")
+    out_rows = out.rearrange("b h w c -> (b h w) c")
+    nm_flat = noise_map.rearrange("b h w o -> (b h w o)")
+
+    with ExitStack() as ctx:
+        ctx.enter_context(tc.manual_schedule())
+        const = ctx.enter_context(tc.tile_pool(name="const", bufs=1))
+        xpool = ctx.enter_context(tc.tile_pool(name="xpool", bufs=NG))
+        mpool = ctx.enter_context(tc.tile_pool(name="mpool", bufs=NG))
+        gpool = ctx.enter_context(tc.tile_pool(name="gpool", bufs=3))
+        spool = ctx.enter_context(tc.tile_pool(name="spool", bufs=5))
+        opool = ctx.enter_context(tc.tile_pool(name="opool", bufs=3))
+        psx = ctx.enter_context(tc.psum_pool(name="psx", bufs=2))
+        psp = ctx.enter_context(tc.psum_pool(name="psp", bufs=4))
+        pso = ctx.enter_context(tc.psum_pool(name="pso", bufs=2))
+
+        ident_f = const.tile([P, P], F32, name="ident_f")
+        make_identity(nc, ident_f[:])
+        eps_t = const.tile([P, 1], F32, name="eps_t")
+        nc.vector.memset(eps_t[:], EPS)
+        vrows = const.tile([P, P], BF16, name="vrows")
+        nc.vector.memset(vrows[:], 0.0)
+        warm = const.tile([P, 1], F32, name="warm")
+        nc.scalar.activation(out=warm[:], in_=eps_t[:], func=ACT.Abs_reciprocal_sqrt)
+        ident_b = const.tile([P, P], BF16, name="ident_b")
+        nc.vector.tensor_copy(out=ident_b[:], in_=ident_f[:])
+
+        x_sb = []
+
+        def load_x(g):
+            t = xpool.tile([P, 4 * CIN], BF16, name="x_sb")
+            nc.sync.dma_start(
+                out=t[:],
+                in_=x_rows[GP * g : GP * (g + 1), :].rearrange("(p j) k -> p (j k)", j=4),
+            )
+            x_sb.append(t)
+
+        nm_t = []
+
+        def load_nm(q):
+            t = const.tile([P, 2048], BF16, name="nm%d" % q)
+            nc.sync.dma_start(
+                out=t[:], in_=nm_flat[2048 * q : 2048 * (q + 1)].partition_broadcast(P)
+            )
+            nm_t.append(t)
+
+        load_x(0)
+        nc.sync.dma_start(
+            out=vrows[0:2, :], in_=noise_weight.rearrange("a b c (h n) -> (a b c h) n", h=2)
+        )
+        nc.sync.dma_start(out=vrows[2:4, :], in_=bias.rearrange("a b c (h n) -> (a b c h) n", h=2))
+        nc.sync.dma_start(out=vrows[4:8, :], in_=dense_b.rearrange("(h n) -> h n", h=4))
+        w_raw = const.tile([P, 4 * NF], BF16, name="w_raw")
+        nc.sync.dma_start(
+            out=w_raw[:].rearrange("i (u r) -> i u r", u=2),
+            in_=conv_w.rearrange("(u i e) c -> i u (e c)", u=2, e=2),
+        )
+        load_nm(0)
+        load_x(1)
+        load_x(2)
+        dl_sb = const.tile([P, 512], BF16, name="dl_sb")
+        nc.sync.dma_start(out=dl_sb[:], in_=dlatents)
+        dw_sb = const.tile([P, 2048], BF16, name="dw_sb")
+        nc.sync.dma_start(
+            out=dw_sb[:].rearrange("p (kb n) -> p kb n", kb=4),
+            in_=dense_w.rearrange("(kb p) n -> p kb n", p=P),
+        )
+        load_x(3)
+        load_nm(1)
+        load_x(4)
+        load_x(5)
+        load_nm(2)
+        load_x(6)
+        load_x(7)
+        load_nm(3)
+        for g in range(8, NG):
+            load_x(g)
+
+        vps = pso.tile([P, P], BF16, name="vps", tag="ot")
+        nc.tensor.transpose(vps[:], vrows[:], ident_b[:])
+        vec = const.tile([P, 8], F32, name="vec")
+        nc.vector.tensor_copy(out=vec[:], in_=vps[:, 0:8])
+        one_g = const.tile([P, 2], F32, name="one_g")
+        nc.vector.tensor_scalar_add(out=one_g[:], in0=vec[:, 4:6], scalar1=1.0)
+
+        w_grp = const.tile([P, 4 * NF], BF16, name="w_grp", align_bytes=64)
+        nc.vector.tensor_copy(
+            out=w_grp[:].rearrange("i (c t) -> i c t", t=4),
+            in_=w_raw[:].rearrange("i (t c) -> i c t", t=4),
+        )
+        w_codes = const.tile([P, NF], U32, name="w_codes", align_bytes=64)
+        w_scl = const.tile([P, NF], U8, name="w_scl", align_bytes=64)
+        nc.vector.quantize_mx(out=w_codes[:].bitcast(FP8X4), scales=w_scl[:], in_=w_grp[:])
+
+        m_sb = {}
+
+        def noise(g):
+            t = mpool.tile([P, 2 * GP], F32, name="m_sb")
+            src = nm_t[g // 4][:, GP * (g % 4) : GP * (g % 4 + 1)].rearrange("c (p j) -> c j p", j=4)
+            for h in range(2):
+                nc.gpsimd.tensor_scalar(
+                    out=t[:, GP * h : GP * (h + 1)].rearrange("c (j p) -> c j p", j=4),
+                    in0=src,
+                    scalar1=vec[:, h : h + 1],
+                    scalar2=vec[:, 2 + h : 3 + h],
+                    op0=ALU.mult,
+                    op1=ALU.add,
+                )
+            m_sb[g] = t
+
+        g1 = const.tile([P, 2 * P], F32, name="g1")
+        bt = const.tile([P, 2 * P], F32, name="bt")
+        dl_t = const.tile([P, 512], BF16, name="dl_t")
+        style_ps = {}
+
+        def style_transposes():
+            dl_ps = pso.tile([P, 512], BF16, name="dl_ps", tag="ot")
+            for kb in range(4):
+                nc.tensor.transpose(
+                    dl_ps[:, P * kb : P * (kb + 1)], dl_sb[:, P * kb : P * (kb + 1)], ident_b[:]
+                )
+            style_ps["dl"] = dl_ps
+
+        def style_copy():
+            nc.vector.tensor_copy(out=dl_t[:], in_=style_ps["dl"][:])
+
+        def style_matmuls():
+            gb = pso.tile([P, 512], F32, name="gb", tag="ot")
+            for cb in range(4):
+                for kb in range(4):
+                    nc.tensor.matmul(
+                        out=gb[:, P * cb : P * (cb + 1)],
+                        lhsT=dw_sb[:, 512 * kb + P * cb : 512 * kb + P * (cb + 1)],
+                        rhs=dl_t[:, P * kb : P * (kb + 1)],
+                        start=(kb == 0),
+                        stop=(kb == 3),
+                    )
+            g1v = g1[:].rearrange("c (g h s) -> c h g s", h=2, s=8)
+            btv = bt[:].rearrange("c (g h s) -> c h g s", h=2, s=8)
+            for h in range(2):
+                nc.scalar.activation(
+                    out=g1v[:, h],
+                    in_=gb[:, P * h : P * (h + 1)].rearrange("c (g s) -> c g s", s=8),
+                    func=ACT.Identity,
+                    bias=one_g[:, h : h + 1],
+                )
+                nc.scalar.activation(
+                    out=btv[:, h],
+                    in_=gb[:, P * (2 + h) : P * (3 + h)].rearrange("c (g s) -> c g s", s=8),
+                    func=ACT.Identity,
+                    bias=vec[:, 6 + h : 7 + h],
+                )
+
+        xts = {}
+        grp = {}
+        prod = {}
+        stats = {}
+        rstd = {}
+        coef = {}
+
+        def t_in(g):
+            x32 = x_sb[g][:].bitcast(F32)
+            banks = []
+            for jj in range(2):
+                xt = psx.tile([P, 512], F32, name="xt")
+                for u in range(2):
+                    for j2 in range(2):
+                        j = 2 * jj + j2
+                        nc.tensor.transpose(
+                            xt[:, 256 * u + P * j2 : 256 * u + P * (j2 + 1)],
+                            x32[:, 256 * j + P * u : 256 * j + P * (u + 1)],
+                            ident_f[:],
+                        )
+                banks.append(xt)
+            xts[g] = banks
+
+        def x_out(g):
+            t = gpool.tile([P, 4 * GP], BF16, name="grp", align_bytes=64)
+            t32 = t[:].bitcast(F32)
+            for jj in range(2):
+                nc.scalar.copy(
+                    out=t32[:, 512 * jj : 512 * (jj + 1)].rearrange("p (c u) -> p c u", u=2),
+                    in_=xts[g][jj][:].rearrange("p (u c) -> p c u", u=2),
+                )
+            grp[g] = t
+
+        def quant_mx(g):
+            cd = gpool.tile([P, GP], U32, name="codes", align_bytes=64)
+            sc = gpool.tile([P, GP], U8, name="scl", align_bytes=64)
+            nc.vector.quantize_mx(out=cd[:].bitcast(FP8X4), scales=sc[:], in_=grp[g][:])
+            pp = []
+            for h in range(2):
+                acc = psp.tile([P, GP], F32, name="acc")
+                nc.tensor.matmul_mx(
+                    out=acc[:],
+                    lhsT=w_codes[:, P * h : P * (h + 1)].bitcast(FP8X4),
+                    lhsT_scale=w_scl[:, P * h : P * (h + 1)],
+                    rhs=cd[:].bitcast(FP8X4),
+                    rhs_scale=sc[:],
+                    start=True,
+                    stop=True,
+                )
+                pp.append(acc)
+            prod[g] = pp
+
+        def add_noise(g):
+            t = m_sb[g]
+            for h in range(2):
+                nc.vector.tensor_tensor(
+                    out=t[:, GP * h : GP * (h + 1)],
+                    in0=prod[g][h][:],
+                    in1=t[:, GP * h : GP * (h + 1)],
+                    op=ALU.add,
+                )
+
+        def lrelu(g):
+            t = m_sb[g]
+            for h in range(2):
+                th = t[:, GP * h : GP * (h + 1)]
+                nc.vector.scalar_tensor_tensor(
+                    out=th, in0=th, scalar=SLOPE, in1=th, op0=ALU.mult, op1=ALU.max
+                )
+
+        def moments(g):
+            t = m_sb[g]
+            st = spool.tile([P, 48], F32, name="st")
+            for h in range(2):
+                yv = t[:, GP * h : GP * (h + 1)].rearrange(
+                    "c (j sp s2 q) -> c sp j q s2", j=4, sp=4, s2=2, q=16
+                )
+                for sp in range(4):
+                    idx = h * 4 + sp
+                    nc.vector.bn_stats(out=st[:, 6 * idx : 6 * idx + 6], in_=yv[:, sp])
+            stats[g] = st
+
+        def inv_std(g):
+            st3 = stats[g][:].rearrange("c (n k) -> c n k", k=3)
+            rs = spool.tile([P, 16], F32, name="rs")
+            nc.scalar.activation(
+                out=rs[:],
+                in_=st3[:, :, 2],
+                func=ACT.Abs_reciprocal_sqrt,
+                scale=1.0 / 64.0,
+                bias=eps_t[:],
+            )
+            rstd[g] = rs
+
+        def coefficients(g, eng):
+            st3 = stats[g][:].rearrange("c (n k) -> c n k", k=3)
+            a_t = spool.tile([P, 16], F32, name="a_t")
+            eng.tensor_tensor(
+                out=a_t[:], in0=rstd[g][:], in1=g1[:, 16 * g : 16 * (g + 1)], op=ALU.mult
+            )
+            ma = spool.tile([P, 16], F32, name="ma")
+            eng.tensor_tensor(out=ma[:], in0=st3[:, :, 1], in1=a_t[:], op=ALU.mult)
+            b_t = spool.tile([P, 16], F32, name="b_t")
+            eng.tensor_tensor(
+                out=b_t[:], in0=bt[:, 16 * g : 16 * (g + 1)], in1=ma[:], op=ALU.subtract
+            )
+            coef[g] = (a_t, b_t)
+
+        def back(g, split):
+            a_t, b_t = coef[g]
+            t = m_sb[g]
+            for h in range(2):
+                yv = t[:, GP * h : GP * (h + 1)].rearrange("c (j s q) -> c s j q", j=4, s=8, q=16)
+                for s in range(8):
+                    lc = 8 * h + s
+                    if split and h == 1:
+                        nc.vector.tensor_scalar(
+                            out=yv[:, s],
+                            in0=yv[:, s],
+                            scalar1=a_t[:, lc : lc + 1],
+                            scalar2=b_t[:, lc : lc + 1],
+                            op0=ALU.mult,
+                            op1=ALU.add,
+                        )
+                    else:
+                        nc.scalar.activation(
+                            out=yv[:, s],
+                            in_=yv[:, s],
+                            func=ACT.Identity,
+                            scale=a_t[:, lc : lc + 1],
+                            bias=b_t[:, lc : lc + 1],
+                        )
+            o_sb = opool.tile([P, 4 * NF], F32, name="o_sb")
+            ov = o_sb[:].rearrange("p (j c) -> p j c", c=NF)
+            banks = []
+            for h in range(2):
+                ot = pso.tile([P, 512], F32, name="ot")
+                for j in range(4):
+                    nc.tensor.transpose(
+                        ot[:, P * j : P * (j + 1)],
+                        t[:, GP * h + P * j : GP * h + P * (j + 1)],
+                        ident_f[:],
+                    )
+                banks.append(ot)
+            for h in range(2):
+                dst = ov[:, :, P * h : P * (h + 1)]
+                src = banks[h][:].rearrange("p (j c) -> p j c", c=P)
+                if split and h == 1:
+                    nc.vector.tensor_copy(out=dst, in_=src)
+                else:
+                    nc.scalar.copy(out=dst, in_=src)
+            nc.sync.dma_start(
+                out=out_rows[GP * g : GP * (g + 1), :].rearrange("(p j) c -> p (j c)", j=4),
+                in_=o_sb[:],
+            )
+
+        for g in range(4):
+            noise(g)
+        t_in(0)
+        x_out(0)
+        t_in(1)
+        x_out(1)
+        quant_mx(0)
+        t_in(2)
+        for i in range(NG + 2):
+            if i + 2 < NG:
+                x_out(i + 2)
+            if i < NG:
+                add_noise(i)
+            if i + 1 < NG:
+                quant_mx(i + 1)
+            if i == 0:
+                style_transposes()
+            if i == 1:
+                style_matmuls()
+            if i < NG:
+                lrelu(i)
+            if i == 0:
+                style_copy()
+            if 1 <= i <= NG:
+                coefficients(i - 1, nc.vector if i == NG else nc.gpsimd)
+            if i + 4 < NG:
+                noise(i + 4)
+            if i < NG:
+                moments(i)
+            if i >= 2:
+                back(i - 2, i >= NG)
+            if i + 3 < NG:
+                t_in(i + 3)
+            if i < NG:
+                inv_std(i)

@@ -34,7 +34,7 @@ def tile_styleganlayerepilogue_t_kernel(
         ctx.enter_context(tc.manual_schedule())
         const = ctx.enter_context(tc.tile_pool(name="const", bufs=1))
         xpool = ctx.enter_context(tc.tile_pool(name="xpool", bufs=NG))
-        mpool = ctx.enter_context(tc.tile_pool(name="mpool", bufs=NG))
+        upool = ctx.enter_context(tc.tile_pool(name="upool", bufs=6))
         gpool = ctx.enter_context(tc.tile_pool(name="gpool", bufs=3))
         spool = ctx.enter_context(tc.tile_pool(name="spool", bufs=5))
         opool = ctx.enter_context(tc.tile_pool(name="opool", bufs=3))
@@ -110,6 +110,8 @@ def tile_styleganlayerepilogue_t_kernel(
         nc.vector.tensor_copy(out=vec[:], in_=vps[:, 0:8])
         one_g = const.tile([P, 2], F32, name="one_g")
         nc.vector.tensor_scalar_add(out=one_g[:], in0=vec[:, 4:6], scalar1=1.0)
+        nb8 = const.tile([P, 2], F32, name="nb8")
+        nc.vector.tensor_scalar_mul(out=nb8[:], in0=vec[:, 2:4], scalar1=SLOPE - 1.0)
 
         w_grp = const.tile([P, 4 * NF], BF16, name="w_grp", align_bytes=64)
         nc.vector.tensor_copy(
@@ -121,20 +123,6 @@ def tile_styleganlayerepilogue_t_kernel(
         nc.vector.quantize_mx(out=w_codes[:].bitcast(FP8X4), scales=w_scl[:], in_=w_grp[:])
 
         m_sb = {}
-
-        def noise(g):
-            t = mpool.tile([P, 2 * GP], F32, name="m_sb")
-            src = nm_t[g // 4][:, GP * (g % 4) : GP * (g % 4 + 1)].rearrange("c (p j) -> c j p", j=4)
-            for h in range(2):
-                nc.gpsimd.tensor_scalar(
-                    out=t[:, GP * h : GP * (h + 1)].rearrange("c (j p) -> c j p", j=4),
-                    in0=src,
-                    scalar1=vec[:, h : h + 1],
-                    scalar2=vec[:, 2 + h : 3 + h],
-                    op0=ALU.mult,
-                    op1=ALU.add,
-                )
-            m_sb[g] = t
 
         g1 = const.tile([P, 2 * P], F32, name="g1")
         bt = const.tile([P, 2 * P], F32, name="bt")
@@ -232,22 +220,34 @@ def tile_styleganlayerepilogue_t_kernel(
             prod[g] = pp
 
         def add_noise(g):
-            t = m_sb[g]
+            t = upool.tile([P, 2 * GP], F32, name="u_sb")
+            src = nm_t[g // 4][:, GP * (g % 4) : GP * (g % 4 + 1)].rearrange("c (p j) -> c j p", j=4)
             for h in range(2):
-                nc.vector.tensor_tensor(
-                    out=t[:, GP * h : GP * (h + 1)],
-                    in0=prod[g][h][:],
-                    in1=t[:, GP * h : GP * (h + 1)],
-                    op=ALU.add,
+                nc.vector.scalar_tensor_tensor(
+                    out=t[:, GP * h : GP * (h + 1)].rearrange("c (j p) -> c j p", j=4),
+                    in0=src,
+                    scalar=vec[:, h : h + 1],
+                    in1=prod[g][h][:].rearrange("c (j p) -> c j p", j=4),
+                    op0=ALU.mult,
+                    op1=ALU.add,
                 )
+            m_sb[g] = t
 
         def lrelu(g):
             t = m_sb[g]
+            v = gpool.tile([P, 2 * GP], F32, name="v_sb")
+            for h in range(2):
+                nc.vector.tensor_scalar(
+                    out=v[:, GP * h : GP * (h + 1)],
+                    in0=t[:, GP * h : GP * (h + 1)],
+                    scalar1=SLOPE,
+                    scalar2=nb8[:, h : h + 1],
+                    op0=ALU.mult,
+                    op1=ALU.add,
+                )
             for h in range(2):
                 th = t[:, GP * h : GP * (h + 1)]
-                nc.vector.scalar_tensor_tensor(
-                    out=th, in0=th, scalar=SLOPE, in1=th, op0=ALU.mult, op1=ALU.max
-                )
+                nc.vector.tensor_tensor(out=th, in0=th, in1=v[:, GP * h : GP * (h + 1)], op=ALU.max)
 
         def moments(g):
             t = m_sb[g]
@@ -287,32 +287,34 @@ def tile_styleganlayerepilogue_t_kernel(
             )
             coef[g] = (a_t, b_t)
 
-        def back(g, split):
+        def affine(g, h, eng):
             a_t, b_t = coef[g]
+            yv = m_sb[g][:, GP * h : GP * (h + 1)].rearrange("c (j s q) -> c s j q", j=4, s=8, q=16)
+            for s in range(8):
+                lc = 8 * h + s
+                if eng == "v":
+                    nc.vector.tensor_scalar(
+                        out=yv[:, s],
+                        in0=yv[:, s],
+                        scalar1=a_t[:, lc : lc + 1],
+                        scalar2=b_t[:, lc : lc + 1],
+                        op0=ALU.mult,
+                        op1=ALU.add,
+                    )
+                else:
+                    nc.scalar.activation(
+                        out=yv[:, s],
+                        in_=yv[:, s],
+                        func=ACT.Identity,
+                        scale=a_t[:, lc : lc + 1],
+                        bias=b_t[:, lc : lc + 1],
+                    )
+
+        ots = {}
+        o_sbs = {}
+
+        def t_back(g):
             t = m_sb[g]
-            for h in range(2):
-                yv = t[:, GP * h : GP * (h + 1)].rearrange("c (j s q) -> c s j q", j=4, s=8, q=16)
-                for s in range(8):
-                    lc = 8 * h + s
-                    if split and h == 1:
-                        nc.vector.tensor_scalar(
-                            out=yv[:, s],
-                            in0=yv[:, s],
-                            scalar1=a_t[:, lc : lc + 1],
-                            scalar2=b_t[:, lc : lc + 1],
-                            op0=ALU.mult,
-                            op1=ALU.add,
-                        )
-                    else:
-                        nc.scalar.activation(
-                            out=yv[:, s],
-                            in_=yv[:, s],
-                            func=ACT.Identity,
-                            scale=a_t[:, lc : lc + 1],
-                            bias=b_t[:, lc : lc + 1],
-                        )
-            o_sb = opool.tile([P, 4 * NF], F32, name="o_sb")
-            ov = o_sb[:].rearrange("p (j c) -> p j c", c=NF)
             banks = []
             for h in range(2):
                 ot = pso.tile([P, 512], F32, name="ot")
@@ -323,50 +325,73 @@ def tile_styleganlayerepilogue_t_kernel(
                         ident_f[:],
                     )
                 banks.append(ot)
-            for h in range(2):
-                dst = ov[:, :, P * h : P * (h + 1)]
-                src = banks[h][:].rearrange("p (j c) -> p j c", c=P)
-                if split and h == 1:
-                    nc.vector.tensor_copy(out=dst, in_=src)
-                else:
-                    nc.scalar.copy(out=dst, in_=src)
+            ots[g] = banks
+            o_sbs[g] = opool.tile([P, 4 * NF], F32, name="o_sb")
+
+        def x2(g, h, eng):
+            dst = o_sbs[g][:].rearrange("p (j c) -> p j c", c=NF)[:, :, P * h : P * (h + 1)]
+            src = ots[g][h][:].rearrange("p (j c) -> p j c", c=P)
+            if eng == "v":
+                nc.vector.tensor_copy(out=dst, in_=src)
+            else:
+                nc.scalar.copy(out=dst, in_=src)
+
+        def store(g):
             nc.sync.dma_start(
                 out=out_rows[GP * g : GP * (g + 1), :].rearrange("(p j) c -> p (j c)", j=4),
-                in_=o_sb[:],
+                in_=o_sbs[g][:],
             )
 
-        for g in range(4):
-            noise(g)
         t_in(0)
         x_out(0)
         t_in(1)
         x_out(1)
         quant_mx(0)
         t_in(2)
-        for i in range(NG + 2):
+        for i in range(NG):
+            if i >= 3:
+                t_back(i - 3)
             if i + 2 < NG:
                 x_out(i + 2)
-            if i < NG:
-                add_noise(i)
+            if i + 3 < NG:
+                t_in(i + 3)
+            add_noise(i)
             if i + 1 < NG:
                 quant_mx(i + 1)
             if i == 0:
                 style_transposes()
             if i == 1:
                 style_matmuls()
-            if i < NG:
-                lrelu(i)
+            if i >= 3:
+                x2(i - 3, 0, "s")
+                x2(i - 3, 1, "s")
+                store(i - 3)
+            lrelu(i)
             if i == 0:
                 style_copy()
-            if 1 <= i <= NG:
-                coefficients(i - 1, nc.vector if i == NG else nc.gpsimd)
-            if i + 4 < NG:
-                noise(i + 4)
-            if i < NG:
-                moments(i)
+            if i >= 1:
+                coefficients(i - 1, nc.gpsimd)
+            moments(i)
             if i >= 2:
-                back(i - 2, i >= NG)
-            if i + 3 < NG:
-                t_in(i + 3)
-            if i < NG:
-                inv_std(i)
+                affine(i - 2, 0, "s")
+                affine(i - 2, 1, "s")
+            if i == NG - 1:
+                affine(NG - 2, 0, "s")
+                affine(NG - 2, 1, "s")
+            inv_std(i)
+        last = NG - 1
+        t_back(last - 2)
+        coefficients(last, nc.vector)
+        x2(last - 2, 0, "s")
+        affine(last, 1, "v")
+        affine(last, 0, "s")
+        x2(last - 2, 1, "v")
+        store(last - 2)
+        t_back(last - 1)
+        x2(last - 1, 0, "s")
+        x2(last - 1, 1, "v")
+        store(last - 1)
+        t_back(last)
+        x2(last, 0, "s")
+        x2(last, 1, "v")
+        store(last)

@@ -35,6 +35,7 @@ def tile_styleganlayerepilogue_t_kernel(
         const = ctx.enter_context(tc.tile_pool(name="const", bufs=1))
         xpool = ctx.enter_context(tc.tile_pool(name="xpool", bufs=NG))
         upool = ctx.enter_context(tc.tile_pool(name="upool", bufs=6))
+        mpool = ctx.enter_context(tc.tile_pool(name="mpool", bufs=2))
         gpool = ctx.enter_context(tc.tile_pool(name="gpool", bufs=3))
         spool = ctx.enter_context(tc.tile_pool(name="spool", bufs=5))
         opool = ctx.enter_context(tc.tile_pool(name="opool", bufs=3))
@@ -110,8 +111,6 @@ def tile_styleganlayerepilogue_t_kernel(
         nc.vector.tensor_copy(out=vec[:], in_=vps[:, 0:8])
         one_g = const.tile([P, 2], F32, name="one_g")
         nc.vector.tensor_scalar_add(out=one_g[:], in0=vec[:, 4:6], scalar1=1.0)
-        nb8 = const.tile([P, 2], F32, name="nb8")
-        nc.vector.tensor_scalar_mul(out=nb8[:], in0=vec[:, 2:4], scalar1=SLOPE - 1.0)
 
         w_grp = const.tile([P, 4 * NF], BF16, name="w_grp", align_bytes=64)
         nc.vector.tensor_copy(
@@ -123,6 +122,21 @@ def tile_styleganlayerepilogue_t_kernel(
         nc.vector.quantize_mx(out=w_codes[:].bitcast(FP8X4), scales=w_scl[:], in_=w_grp[:])
 
         m_sb = {}
+        z_sb = {}
+
+        def noise(g):
+            t = mpool.tile([P, 2 * GP], F32, name="z_sb")
+            src = nm_t[g // 4][:, GP * (g % 4) : GP * (g % 4 + 1)].rearrange("c (p j) -> c j p", j=4)
+            for h in range(2):
+                nc.gpsimd.tensor_scalar(
+                    out=t[:, GP * h : GP * (h + 1)].rearrange("c (j p) -> c j p", j=4),
+                    in0=src,
+                    scalar1=vec[:, h : h + 1],
+                    scalar2=vec[:, 2 + h : 3 + h],
+                    op0=ALU.mult,
+                    op1=ALU.add,
+                )
+            z_sb[g] = t
 
         g1 = const.tile([P, 2 * P], F32, name="g1")
         bt = const.tile([P, 2 * P], F32, name="bt")
@@ -220,34 +234,29 @@ def tile_styleganlayerepilogue_t_kernel(
             prod[g] = pp
 
         def add_noise(g):
-            t = upool.tile([P, 2 * GP], F32, name="u_sb")
-            src = nm_t[g // 4][:, GP * (g % 4) : GP * (g % 4 + 1)].rearrange("c (p j) -> c j p", j=4)
+            t = z_sb[g]
             for h in range(2):
-                nc.vector.scalar_tensor_tensor(
-                    out=t[:, GP * h : GP * (h + 1)].rearrange("c (j p) -> c j p", j=4),
-                    in0=src,
-                    scalar=vec[:, h : h + 1],
-                    in1=prod[g][h][:].rearrange("c (j p) -> c j p", j=4),
-                    op0=ALU.mult,
-                    op1=ALU.add,
+                nc.vector.tensor_tensor(
+                    out=t[:, GP * h : GP * (h + 1)],
+                    in0=prod[g][h][:],
+                    in1=t[:, GP * h : GP * (h + 1)],
+                    op=ALU.add,
                 )
-            m_sb[g] = t
 
         def lrelu(g):
-            t = m_sb[g]
-            v = gpool.tile([P, 2 * GP], F32, name="v_sb")
+            z = z_sb[g]
+            t = upool.tile([P, 2 * GP], F32, name="y_sb")
             for h in range(2):
-                nc.vector.tensor_scalar(
-                    out=v[:, GP * h : GP * (h + 1)],
-                    in0=t[:, GP * h : GP * (h + 1)],
-                    scalar1=SLOPE,
-                    scalar2=nb8[:, h : h + 1],
+                zh = z[:, GP * h : GP * (h + 1)]
+                nc.vector.scalar_tensor_tensor(
+                    out=t[:, GP * h : GP * (h + 1)],
+                    in0=zh,
+                    scalar=SLOPE,
+                    in1=zh,
                     op0=ALU.mult,
-                    op1=ALU.add,
+                    op1=ALU.max,
                 )
-            for h in range(2):
-                th = t[:, GP * h : GP * (h + 1)]
-                nc.vector.tensor_tensor(out=th, in0=th, in1=v[:, GP * h : GP * (h + 1)], op=ALU.max)
+            m_sb[g] = t
 
         def moments(g):
             t = m_sb[g]
@@ -342,6 +351,8 @@ def tile_styleganlayerepilogue_t_kernel(
                 in_=o_sbs[g][:],
             )
 
+        noise(0)
+        noise(1)
         t_in(0)
         x_out(0)
         t_in(1)
@@ -371,6 +382,8 @@ def tile_styleganlayerepilogue_t_kernel(
                 style_copy()
             if i >= 1:
                 coefficients(i - 1, nc.gpsimd)
+            if i + 2 < NG:
+                noise(i + 2)
             moments(i)
             if i >= 2:
                 affine(i - 2, 0, "s")

@@ -40,7 +40,8 @@ def tile_styleganlayerepilogue_t_kernel(
         spool = ctx.enter_context(tc.tile_pool(name="spool", bufs=5))
         opool = ctx.enter_context(tc.tile_pool(name="opool", bufs=3))
         psx = ctx.enter_context(tc.psum_pool(name="psx", bufs=2))
-        psp = ctx.enter_context(tc.psum_pool(name="psp", bufs=4))
+        psp = ctx.enter_context(tc.psum_pool(name="psp", bufs=2))
+        psn = ctx.enter_context(tc.psum_pool(name="psn", bufs=2))
         pso = ctx.enter_context(tc.psum_pool(name="pso", bufs=2))
 
         ident_f = const.tile([P, P], F32, name="ident_f")
@@ -49,8 +50,6 @@ def tile_styleganlayerepilogue_t_kernel(
         nc.vector.memset(eps_t[:], EPS)
         vrows = const.tile([P, P], BF16, name="vrows")
         nc.vector.memset(vrows[:], 0.0)
-        warm = const.tile([P, 1], F32, name="warm")
-        nc.scalar.activation(out=warm[:], in_=eps_t[:], func=ACT.Abs_reciprocal_sqrt)
         ident_b = const.tile([P, P], BF16, name="ident_b")
         nc.vector.tensor_copy(out=ident_b[:], in_=ident_f[:])
 
@@ -64,27 +63,18 @@ def tile_styleganlayerepilogue_t_kernel(
             )
             x_sb.append(t)
 
-        nm_t = []
-
-        def load_nm(q):
-            t = const.tile([P, 2048], BF16, name="nm%d" % q)
-            nc.sync.dma_start(
-                out=t[:], in_=nm_flat[2048 * q : 2048 * (q + 1)].partition_broadcast(P)
-            )
-            nm_t.append(t)
-
-        load_x(0)
-        nc.sync.dma_start(
+        nc.scalar.dma_start(
             out=vrows[0:2, :], in_=noise_weight.rearrange("a b c (h n) -> (a b c h) n", h=2)
         )
-        nc.sync.dma_start(out=vrows[2:4, :], in_=bias.rearrange("a b c (h n) -> (a b c h) n", h=2))
-        nc.sync.dma_start(out=vrows[4:8, :], in_=dense_b.rearrange("(h n) -> h n", h=4))
+        nc.scalar.dma_start(out=vrows[2:4, :], in_=bias.rearrange("a b c (h n) -> (a b c h) n", h=2))
+        nc.scalar.dma_start(out=vrows[64:128, :], in_=nm_flat.rearrange("(r n) -> r n", n=P))
+        nc.scalar.dma_start(out=vrows[4:8, :], in_=dense_b.rearrange("(h n) -> h n", h=4))
+        load_x(0)
         w_raw = const.tile([P, 4 * NF], BF16, name="w_raw")
         nc.sync.dma_start(
             out=w_raw[:].rearrange("i (u r) -> i u r", u=2),
             in_=conv_w.rearrange("(u i e) c -> i u (e c)", u=2, e=2),
         )
-        load_nm(0)
         load_x(1)
         load_x(2)
         dl_sb = const.tile([P, 512], BF16, name="dl_sb")
@@ -94,21 +84,18 @@ def tile_styleganlayerepilogue_t_kernel(
             out=dw_sb[:].rearrange("p (kb n) -> p kb n", kb=4),
             in_=dense_w.rearrange("(kb p) n -> p kb n", p=P),
         )
-        load_x(3)
-        load_nm(1)
-        load_x(4)
-        load_x(5)
-        load_nm(2)
-        load_x(6)
-        load_x(7)
-        load_nm(3)
-        for g in range(8, NG):
+        for g in range(3, NG):
             load_x(g)
+
+        warm = const.tile([P, 1], F32, name="warm")
+        nc.scalar.activation(out=warm[:], in_=eps_t[:], func=ACT.Abs_reciprocal_sqrt)
 
         vps = pso.tile([P, P], BF16, name="vps", tag="ot")
         nc.tensor.transpose(vps[:], vrows[:], ident_b[:])
         vec = const.tile([P, 8], F32, name="vec")
         nc.vector.tensor_copy(out=vec[:], in_=vps[:, 0:8])
+        nm_col = const.tile([P, 64], BF16, name="nm_col")
+        nc.vector.tensor_copy(out=nm_col[:], in_=vps[:, 64:128])
         one_g = const.tile([P, 2], F32, name="one_g")
         nc.vector.tensor_scalar_add(out=one_g[:], in0=vec[:, 4:6], scalar1=1.0)
 
@@ -124,9 +111,27 @@ def tile_styleganlayerepilogue_t_kernel(
         m_sb = {}
         z_sb = {}
 
+        nbs = {}
+        nmb = {}
+
+        def bcast(g):
+            nb = psn.tile([P, GP], BF16, name="nb")
+            for r in range(4):
+                nc.tensor.transpose(
+                    nb[:, P * r : P * (r + 1)],
+                    nm_col[:, 4 * g + r : 4 * g + r + 1].to_broadcast([P, P]),
+                    ident_b[:],
+                )
+            nbs[g] = nb
+
+        def nb_out(g):
+            t = gpool.tile([P, GP], BF16, name="nmb")
+            nc.scalar.copy(out=t[:], in_=nbs[g][:])
+            nmb[g] = t
+
         def noise(g):
             t = mpool.tile([P, 2 * GP], F32, name="z_sb")
-            src = nm_t[g // 4][:, GP * (g % 4) : GP * (g % 4 + 1)].rearrange("c (p j) -> c j p", j=4)
+            src = nmb[g][:].rearrange("c (p j) -> c j p", j=4)
             for h in range(2):
                 nc.gpsimd.tensor_scalar(
                     out=t[:, GP * h : GP * (h + 1)].rearrange("c (j p) -> c j p", j=4),
@@ -351,14 +356,20 @@ def tile_styleganlayerepilogue_t_kernel(
                 in_=o_sbs[g][:],
             )
 
+        bcast(0)
+        nb_out(0)
         noise(0)
-        noise(1)
         t_in(0)
         x_out(0)
+        bcast(1)
+        nb_out(1)
+        noise(1)
         t_in(1)
         x_out(1)
         quant_mx(0)
         t_in(2)
+        bcast(2)
+        nb_out(2)
         for i in range(NG):
             if i >= 3:
                 t_back(i - 3)
@@ -366,6 +377,7 @@ def tile_styleganlayerepilogue_t_kernel(
                 x_out(i + 2)
             if i + 3 < NG:
                 t_in(i + 3)
+                bcast(i + 3)
             add_noise(i)
             if i + 1 < NG:
                 quant_mx(i + 1)
@@ -377,6 +389,8 @@ def tile_styleganlayerepilogue_t_kernel(
                 x2(i - 3, 0, "s")
                 x2(i - 3, 1, "s")
                 store(i - 3)
+            if i + 3 < NG:
+                nb_out(i + 3)
             lrelu(i)
             if i == 0:
                 style_copy()

from contextlib import ExitStack

import concourse.mybir as mybir
from concourse.masks import make_identity

F32 = mybir.dt.float32
BF16 = mybir.dt.bfloat16
U32 = mybir.dt.uint32
U8 = mybir.dt.uint8
FP8X4 = mybir.dt.float8_e4m3fn_x4
ALU = mybir.AluOpType
ACT = mybir.ActivationFunctionType

P = 128
PIX = 8192
CIN = 512
NF = 256
GP = 512
NG = PIX // GP
EPS = 1e-8
SLOPE = 0.2
FLOPS = 2 * PIX * CIN * NF + 2 * 128 * 512 * 512


def tile_styleganlayerepilogue_t_kernel(
    tc, x, dlatents, noise_map, conv_w, noise_weight, bias, dense_w, dense_b, out
):
    nc = tc.nc
    x_rows = x.rearrange("b h w k -> (b h w) k")
    out_rows = out.rearrange("b h w c -> (b h w) c")
    nm_flat = noise_map.rearrange("b h w o -> (b h w o)")

    with ExitStack() as ctx:
        ctx.enter_context(tc.manual_schedule())
        const = ctx.enter_context(tc.tile_pool(name="const", bufs=1))
        xpool = ctx.enter_context(tc.tile_pool(name="xpool", bufs=NG))
        upool = ctx.enter_context(tc.tile_pool(name="upool", bufs=6))
        mpool = ctx.enter_context(tc.tile_pool(name="mpool", bufs=2))
        gpool = ctx.enter_context(tc.tile_pool(name="gpool", bufs=3))
        spool = ctx.enter_context(tc.tile_pool(name="spool", bufs=5))
        opool = ctx.enter_context(tc.tile_pool(name="opool", bufs=3))
        psx = ctx.enter_context(tc.psum_pool(name="psx", bufs=2))
        psp = ctx.enter_context(tc.psum_pool(name="psp", bufs=2))
        psn = ctx.enter_context(tc.psum_pool(name="psn", bufs=2))
        pso = ctx.enter_context(tc.psum_pool(name="pso", bufs=2))

        ident_f = const.tile([P, P], F32, name="ident_f")
        make_identity(nc, ident_f[:])
        eps_t = const.tile([P, 1], F32, name="eps_t")
        nc.vector.memset(eps_t[:], EPS)
        vrows = const.tile([P, P], BF16, name="vrows")
        nc.vector.memset(vrows[:], 0.0)
        ident_b = const.tile([P, P], BF16, name="ident_b")
        nc.vector.tensor_copy(out=ident_b[:], in_=ident_f[:])

        x_sb = []

        def load_x(g):
            t = xpool.tile([P, 4 * CIN], BF16, name="x_sb")
            nc.sync.dma_start(
                out=t[:],
                in_=x_rows[GP * g : GP * (g + 1), :].rearrange("(p j) k -> p (j k)", j=4),
            )
            x_sb.append(t)

        nc.scalar.dma_start(
            out=vrows[0:2, :], in_=noise_weight.rearrange("a b c (h n) -> (a b c h) n", h=2)
        )
        nc.scalar.dma_start(out=vrows[2:4, :], in_=bias.rearrange("a b c (h n) -> (a b c h) n", h=2))
        nc.scalar.dma_start(out=vrows[64:128, :], in_=nm_flat.rearrange("(r n) -> r n", n=P))
        nc.scalar.dma_start(out=vrows[4:8, :], in_=dense_b.rearrange("(h n) -> h n", h=4))
        load_x(0)
        w_raw = const.tile([P, 4 * NF], BF16, name="w_raw")
        nc.sync.dma_start(
            out=w_raw[:].rearrange("i (u r) -> i u r", u=2),
            in_=conv_w.rearrange("(u i e) c -> i u (e c)", u=2, e=2),
        )
        load_x(1)
        load_x(2)
        dl_sb = const.tile([P, 512], BF16, name="dl_sb")
        nc.sync.dma_start(out=dl_sb[:], in_=dlatents)
        dw_sb = const.tile([P, 2048], BF16, name="dw_sb")
        nc.sync.dma_start(
            out=dw_sb[:].rearrange("p (kb n) -> p kb n", kb=4),
            in_=dense_w.rearrange("(kb p) n -> p kb n", p=P),
        )
        for g in range(3, NG):
            load_x(g)

        warm = const.tile([P, 1], F32, name="warm")
        nc.scalar.activation(out=warm[:], in_=eps_t[:], func=ACT.Abs_reciprocal_sqrt)

        vps = pso.tile([P, P], BF16, name="vps", tag="ot")
        nc.tensor.transpose(vps[:], vrows[:], ident_b[:])
        vec = const.tile([P, 8], F32, name="vec")
        nc.vector.tensor_copy(out=vec[:], in_=vps[:, 0:8])
        nm_col = const.tile([P, 64], BF16, name="nm_col")
        nc.vector.tensor_copy(out=nm_col[:], in_=vps[:, 64:128])
        one_g = const.tile([P, 2], F32, name="one_g")
        nc.vector.tensor_scalar_add(out=one_g[:], in0=vec[:, 4:6], scalar1=1.0)

        w_grp = const.tile([P, 4 * NF], BF16, name="w_grp", align_bytes=64)
        nc.vector.tensor_copy(
            out=w_grp[:].rearrange("i (c t) -> i c t", t=4),
            in_=w_raw[:].rearrange("i (t c) -> i c t", t=4),
        )
        w_codes = const.tile([P, NF], U32, name="w_codes", align_bytes=64)
        w_scl = const.tile([P, NF], U8, name="w_scl", align_bytes=64)
        nc.vector.quantize_mx(out=w_codes[:].bitcast(FP8X4), scales=w_scl[:], in_=w_grp[:])

        m_sb = {}
        z_sb = {}

        nbs = {}
        nmb = {}

        def bcast(g):
            nb = psn.tile([P, GP], BF16, name="nb")
            for r in range(4):
                nc.tensor.transpose(
                    nb[:, P * r : P * (r + 1)],
                    nm_col[:, 4 * g + r : 4 * g + r + 1].to_broadcast([P, P]),
                    ident_b[:],
                )
            nbs[g] = nb

        def nb_out(g):
            t = gpool.tile([P, GP], BF16, name="nmb")
            nc.scalar.copy(out=t[:], in_=nbs[g][:])
            nmb[g] = t

        def noise(g):
            t = mpool.tile([P, 2 * GP], F32, name="z_sb")
            src = nmb[g][:].rearrange("c (p j) -> c j p", j=4)
            for h in range(2):
                nc.gpsimd.tensor_scalar(
                    out=t[:, GP * h : GP * (h + 1)].rearrange("c (j p) -> c j p", j=4),
                    in0=src,
                    scalar1=vec[:, h : h + 1],
                    scalar2=vec[:, 2 + h : 3 + h],
                    op0=ALU.mult,
                    op1=ALU.add,
                )
            z_sb[g] = t

        g1 = const.tile([P, 2 * P], F32, name="g1")
        bt = const.tile([P, 2 * P], F32, name="bt")
        dl_t = const.tile([P, 512], BF16, name="dl_t")
        style_ps = {}

        def style_transposes():
            dl_ps = pso.tile([P, 512], BF16, name="dl_ps", tag="ot")
            for kb in range(4):
                nc.tensor.transpose(
                    dl_ps[:, P * kb : P * (kb + 1)], dl_sb[:, P * kb : P * (kb + 1)], ident_b[:]
                )
            style_ps["dl"] = dl_ps

        def style_copy():
            nc.vector.tensor_copy(out=dl_t[:], in_=style_ps["dl"][:])

        def style_matmuls():
            gb = pso.tile([P, 512], F32, name="gb", tag="ot")
            for cb in range(4):
                for kb in range(4):
                    nc.tensor.matmul(
                        out=gb[:, P * cb : P * (cb + 1)],
                        lhsT=dw_sb[:, 512 * kb + P * cb : 512 * kb + P * (cb + 1)],
                        rhs=dl_t[:, P * kb : P * (kb + 1)],
                        start=(kb == 0),
                        stop=(kb == 3),
                    )
            g1v = g1[:].rearrange("c (g h s) -> c h g s", h=2, s=8)
            btv = bt[:].rearrange("c (g h s) -> c h g s", h=2, s=8)
            for h in range(2):
                nc.scalar.activation(
                    out=g1v[:, h],
                    in_=gb[:, P * h : P * (h + 1)].rearrange("c (g s) -> c g s", s=8),
                    func=ACT.Identity,
                    bias=one_g[:, h : h + 1],
                )
                nc.scalar.activation(
                    out=btv[:, h],
                    in_=gb[:, P * (2 + h) : P * (3 + h)].rearrange("c (g s) -> c g s", s=8),
                    func=ACT.Identity,
                    bias=vec[:, 6 + h : 7 + h],
                )

        xts = {}
        grp = {}
        prod = {}
        stats = {}
        rstd = {}
        coef = {}

        def t_in(g):
            x32 = x_sb[g][:].bitcast(F32)
            banks = []
            for jj in range(2):
                xt = psx.tile([P, 512], F32, name="xt")
                for u in range(2):
                    for j2 in range(2):
                        j = 2 * jj + j2
                        nc.tensor.transpose(
                            xt[:, 256 * u + P * j2 : 256 * u + P * (j2 + 1)],
                            x32[:, 256 * j + P * u : 256 * j + P * (u + 1)],
                            ident_f[:],
                        )
                banks.append(xt)
            xts[g] = banks

        def x_out(g):
            t = gpool.tile([P, 4 * GP], BF16, name="grp", align_bytes=64)
            t32 = t[:].bitcast(F32)
            for jj in range(2):
                nc.scalar.copy(
                    out=t32[:, 512 * jj : 512 * (jj + 1)].rearrange("p (c u) -> p c u", u=2),
                    in_=xts[g][jj][:].rearrange("p (u c) -> p c u", u=2),
                )
            grp[g] = t

        def quant_mx(g):
            cd = gpool.tile([P, GP], U32, name="codes", align_bytes=64)
            sc = gpool.tile([P, GP], U8, name="scl", align_bytes=64)
            nc.vector.quantize_mx(out=cd[:].bitcast(FP8X4), scales=sc[:], in_=grp[g][:])
            pp = []
            for h in range(2):
                acc = psp.tile([P, GP], F32, name="acc")
                nc.tensor.matmul_mx(
                    out=acc[:],
                    lhsT=w_codes[:, P * h : P * (h + 1)].bitcast(FP8X4),
                    lhsT_scale=w_scl[:, P * h : P * (h + 1)],
                    rhs=cd[:].bitcast(FP8X4),
                    rhs_scale=sc[:],
                    start=True,
                    stop=True,
                )
                pp.append(acc)
            prod[g] = pp

        def add_noise(g):
            t = z_sb[g]
            for h in range(2):
                nc.vector.tensor_tensor(
                    out=t[:, GP * h : GP * (h + 1)],
                    in0=prod[g][h][:],
                    in1=t[:, GP * h : GP * (h + 1)],
                    op=ALU.add,
                )

        def lrelu(g):
            z = z_sb[g]
            t = upool.tile([P, 2 * GP], F32, name="y_sb")
            for h in range(2):
                zh = z[:, GP * h : GP * (h + 1)]
                nc.vector.scalar_tensor_tensor(
                    out=t[:, GP * h : GP * (h + 1)],
                    in0=zh,
                    scalar=SLOPE,
                    in1=zh,
                    op0=ALU.mult,
                    op1=ALU.max,
                )
            m_sb[g] = t

        def moments(g):
            t = m_sb[g]
            st = spool.tile([P, 48], F32, name="st")
            for h in range(2):
                yv = t[:, GP * h : GP * (h + 1)].rearrange(
                    "c (j sp s2 q) -> c sp j q s2", j=4, sp=4, s2=2, q=16
                )
                for sp in range(4):
                    idx = h * 4 + sp
                    nc.vector.bn_stats(out=st[:, 6 * idx : 6 * idx + 6], in_=yv[:, sp])
            stats[g] = st

        def inv_std(g):
            st3 = stats[g][:].rearrange("c (n k) -> c n k", k=3)
            rs = spool.tile([P, 16], F32, name="rs")
            nc.scalar.activation(
                out=rs[:],
                in_=st3[:, :, 2],
                func=ACT.Abs_reciprocal_sqrt,
                scale=1.0 / 64.0,
                bias=eps_t[:],
            )
            rstd[g] = rs

        def coefficients(g, eng):
            st3 = stats[g][:].rearrange("c (n k) -> c n k", k=3)
            a_t = spool.tile([P, 16], F32, name="a_t")
            eng.tensor_tensor(
                out=a_t[:], in0=rstd[g][:], in1=g1[:, 16 * g : 16 * (g + 1)], op=ALU.mult
            )
            ma = spool.tile([P, 16], F32, name="ma")
            eng.tensor_tensor(out=ma[:], in0=st3[:, :, 1], in1=a_t[:], op=ALU.mult)
            b_t = spool.tile([P, 16], F32, name="b_t")
            eng.tensor_tensor(
                out=b_t[:], in0=bt[:, 16 * g : 16 * (g + 1)], in1=ma[:], op=ALU.subtract
            )
            coef[g] = (a_t, b_t)

        def affine(g, h, eng):
            a_t, b_t = coef[g]
            yv = m_sb[g][:, GP * h : GP * (h + 1)].rearrange("c (j s q) -> c s j q", j=4, s=8, q=16)
            for s in range(8):
                lc = 8 * h + s
                if eng == "v":
                    nc.vector.tensor_scalar(
                        out=yv[:, s],
                        in0=yv[:, s],
                        scalar1=a_t[:, lc : lc + 1],
                        scalar2=b_t[:, lc : lc + 1],
                        op0=ALU.mult,
                        op1=ALU.add,
                    )
                else:
                    nc.scalar.activation(
                        out=yv[:, s],
                        in_=yv[:, s],
                        func=ACT.Identity,
                        scale=a_t[:, lc : lc + 1],
                        bias=b_t[:, lc : lc + 1],
                    )

        ots = {}
        o_sbs = {}

        def t_back(g):
            t = m_sb[g]
            banks = []
            for h in range(2):
                ot = pso.tile([P, 512], F32, name="ot")
                for j in range(4):
                    nc.tensor.transpose(
                        ot[:, P * j : P * (j + 1)],
                        t[:, GP * h + P * j : GP * h + P * (j + 1)],
                        ident_f[:],
                    )
                banks.append(ot)
            ots[g] = banks
            o_sbs[g] = opool.tile([P, 4 * NF], F32, name="o_sb")

        def x2(g, h, eng):
            dst = o_sbs[g][:].rearrange("p (j c) -> p j c", c=NF)[:, :, P * h : P * (h + 1)]
            src = ots[g][h][:].rearrange("p (j c) -> p j c", c=P)
            if eng == "v":
                nc.vector.tensor_copy(out=dst, in_=src)
            else:
                nc.scalar.copy(out=dst, in_=src)

        def store(g):
            nc.sync.dma_start(
                out=out_rows[GP * g : GP * (g + 1), :].rearrange("(p j) c -> p (j c)", j=4),
                in_=o_sbs[g][:],
            )

        bcast(0)
        nb_out(0)
        noise(0)
        t_in(0)
        x_out(0)
        bcast(1)
        nb_out(1)
        noise(1)
        t_in(1)
        x_out(1)
        quant_mx(0)
        t_in(2)
        bcast(2)
        nb_out(2)
        for i in range(NG):
            if i >= 3:
                t_back(i - 3)
            if i + 2 < NG:
                x_out(i + 2)
            if i + 3 < NG:
                t_in(i + 3)
                bcast(i + 3)
            add_noise(i)
            if i + 1 < NG:
                quant_mx(i + 1)
            if i == 0:
                style_transposes()
            if i == 1:
                style_matmuls()
            if i >= 3:
                x2(i - 3, 0, "s")
                x2(i - 3, 1, "s")
                store(i - 3)
            if i + 3 < NG:
                nb_out(i + 3)
            lrelu(i)
            if i == 0:
                style_copy()
            if i >= 1:
                coefficients(i - 1, nc.gpsimd)
            if i + 2 < NG:
                noise(i + 2)
            moments(i)
            if i >= 2:
                affine(i - 2, 0, "s")
                affine(i - 2, 1, "s")
            if i == NG - 1:
                affine(NG - 2, 0, "s")
                affine(NG - 2, 1, "s")
            inv_std(i)
        last = NG - 1
        t_back(last - 2)
        coefficients(last, nc.vector)
        x2(last - 2, 0, "s")
        affine(last, 1, "v")
        affine(last, 0, "s")
        x2(last - 2, 1, "v")
        store(last - 2)
        t_back(last - 1)
        x2(last - 1, 0, "s")
        x2(last - 1, 1, "v")
        store(last - 1)
        t_back(last)
        x2(last, 0, "s")
        x2(last, 1, "v")
        store(last)
